import numpy as np
import ml_dtypes


def mxq(x, axis, fmt="e4m3"):
    dtype, down = {"e4m3": (ml_dtypes.float8_e4m3fn, 7), "e5m2": (ml_dtypes.float8_e5m2, 14)}[fmt]
    v = np.moveaxis(np.asarray(x, np.float32).astype(ml_dtypes.bfloat16).astype(np.float64), axis, -1)
    blocks = v.reshape(v.shape[:-1] + (-1, 32))
    amax = np.abs(blocks).max(-1, keepdims=True)
    byte = np.maximum(np.where(amax > 0, np.frexp(amax)[1] - 1 + 127, 0) - down, 1)
    scale = np.exp2(byte - 127.0)
    codes = (blocks / scale).astype(np.float32).astype(dtype).astype(np.float64)
    return np.moveaxis((codes * scale).reshape(v.shape), -1, axis)


WIDE = False


def mx_kscale(k):
    if not WIDE:
        return np.ones(k)
    levels = np.array([10, -10, 5, -5, 0])
    a = np.random.permutation(np.resize(levels, k // 512 * 4)).reshape(k // 512, 4)
    idx = np.arange(k)
    return np.exp2(a[idx // 512, idx % 128 // 32])


BF16 = ml_dtypes.bfloat16


def bf(x):
    return np.asarray(x, np.float32).astype(BF16)


def f64(x):
    return np.asarray(x).astype(np.float64)


M, N, E, P, S, B, KT = 1024, 512, 16, 32, 17, 128, 2


def setup_inputs():
    s = mx_kscale(N)
    eye = np.concatenate([np.eye(N), np.zeros((N, M - N))], axis=1)
    return {
        "context": bf(np.random.standard_normal((S, B, N)) * s),
        "D": bf((eye + np.random.standard_normal((N, M)) * 0.3 / np.sqrt(M)) * s[:, None]),
        "z": bf(np.random.standard_normal((M, B))),
        "conv_w": bf(np.random.standard_normal((N, N, KT)) / np.sqrt(N) / s[None, :, None]),
        "conv_b": bf(np.random.standard_normal(N) * 0.1),
        "t1": bf(np.sqrt(np.sum(s * s)) * (0.5 + 0.1 * np.random.random_sample(1))),
    }


def reference(context, D, z, conv_w, conv_b, t1):
    c = f64(context)
    z_obs = f64(D) @ f64(z)
    distances = np.sum(np.abs(c[:-1] - z_obs.T[None, :, :]), axis=2)
    lg = -distances / f64(t1)[0]
    ex = np.exp(lg - lg.max(axis=0, keepdims=True))
    attn = ex / ex.sum(axis=0, keepdims=True)
    cq = mxq(c, 2, "e4m3")
    w = f64(conv_w)
    encoded = ((cq[:-1] @ mxq(w[:, :, 0], 1, "e4m3").T)
               + (cq[1:] @ mxq(w[:, :, 1], 1, "e4m3").T)
               + f64(conv_b))
    return np.sum(encoded * attn[:, :, None], axis=0)

@@ -1,0 +1,279 @@
+from contextlib import ExitStack
+
+import concourse.mybir as mybir
+from concourse.masks import make_identity
+
+F32 = mybir.dt.float32
+BF16 = mybir.dt.bfloat16
+U32 = mybir.dt.uint32
+U8 = mybir.dt.uint8
+FP8X4 = mybir.dt.float8_e4m3fn_x4
+ALU = mybir.AluOpType
+ACT = mybir.ActivationFunctionType
+AX = mybir.AxisListType
+
+P = 128
+FRAMES = 16
+N = 512
+M = 1024
+FLOPS = 2 * FRAMES * P * N * N * 2 + 2 * N * M * P
+
+EW_ON_SCALAR = (1, 3)
+EC_ON_SCALAR = (0, 6, 7, 8)
+SUB_ON_GPSIMD = (5, 6, 7, 8, 12, 14)
+WS_ON_SCALAR = (1, 4, 7, 8, 10)
+PINNED = True
+LOADS = ("z", "D0", "D1", "D2", "D3", "t", "W0", "W1", "W2", "W3", "c0", "c1", "c2", "c3", "c4", "b")
+C_GROUPS = ((0, 2), (2, 4), (4, 8), (8, 12), (12, 17))
+
+ORDER = (
+    ("TD", 0, 0), ("TD", 0, 1), ("ED", 0, 0), ("ED", 0, 1), ("TD", 1, 0), ("TD", 1, 1),
+    ("ED", 1, 0), ("MZ", 0, 0), ("ED", 1, 1), ("TD", 2, 0), ("TD", 2, 1), ("ED", 2, 0),
+    ("TD", 3, 0), ("ED", 2, 1), ("TD", 3, 1), ("ED", 3, 0), ("MZ", 1, 0), ("ED", 3, 1),
+    ("TW", 0, 0), ("TW", 1, 0), ("EW", 0, 0), ("TW", 2, 0), ("EW", 1, 0), ("TW", 3, 0),
+    ("EW", 2, 0), ("MZ", 2, 0), ("EW", 3, 0), ("MZ", 3, 0), ("TC", 0, 0), ("EZ", 0, 0),
+    ("QW", 0, 0), ("RT", 0, 0), ("TC", 1, 0), ("EC", 0, 0), ("SUB", 0, 0), ("SUB", 5, 0),
+    ("TC", 2, 0), ("SUB", 1, 0), ("ABS", 0, 0), ("TC", 3, 0), ("SUB", 2, 0), ("ABS", 1, 0),
+    ("QW", 1, 0), ("SUB", 6, 0), ("ABS", 2, 0), ("TC", 4, 0), ("TC", 5, 0), ("SUB", 3, 0),
+    ("ABS", 5, 0), ("EC", 1, 0), ("SUB", 7, 0), ("ABS", 3, 0), ("SUB", 4, 0), ("ABS", 6, 0),
+    ("TC", 6, 0), ("EC", 2, 0), ("TC", 7, 0), ("SUB", 8, 0), ("ABS", 4, 0), ("TC", 8, 0),
+    ("QC", 0, 0), ("SUB", 9, 0), ("ABS", 7, 0), ("MX", 0, 0), ("SUB", 10, 0), ("ABS", 9, 0),
+    ("SUB", 12, 0), ("QC", 1, 0), ("ABS", 8, 0), ("SUB", 11, 0), ("ABS", 10, 0), ("SUB", 14, 0),
+    ("EC", 3, 0), ("ABS", 11, 0), ("QC", 2, 0), ("MX", 1, 0), ("SUB", 13, 0), ("ABS", 12, 0),
+    ("QC", 3, 0), ("ABS", 13, 0), ("SUB", 15, 0), ("ABS", 14, 0), ("EC", 4, 0), ("MX", 2, 0),
+    ("QC", 4, 0), ("ABS", 15, 0), ("MX", 3, 0), ("EC", 5, 0), ("EC", 6, 0), ("SM", 1, 0),
+    ("MX", 4, 0), ("QC", 5, 0), ("SM", 2, 0), ("QC", 6, 0), ("EC", 7, 0), ("MX", 5, 0),
+    ("SM", 3, 0), ("WS", 0, 0), ("EC", 8, 0), ("MX", 6, 0), ("WS", 1, 0), ("QC", 7, 0),
+    ("MX", 7, 0), ("QC", 8, 0), ("WS", 4, 0), ("WS", 2, 0), ("MX", 8, 0), ("WS", 7, 0),
+    ("GA", 4, 0), ("WS", 3, 0), ("MX", 9, 0), ("WS", 8, 0), ("WS", 5, 0), ("MX", 10, 0),
+    ("GA", 7, 0), ("WS", 6, 0), ("MX", 11, 0), ("WS", 10, 0), ("WS", 9, 0), ("MX", 12, 0),
+    ("MX", 13, 0), ("WS", 11, 0), ("GA", 8, 0), ("MX", 14, 0), ("WS", 12, 0), ("MX", 15, 0),
+    ("WS", 13, 0), ("GA", 10, 0), ("WS", 14, 0), ("WS", 15, 0), ("MG", 1, 0), ("MG", 2, 0),
+)
+
+
+def tile_dynamix_pa_kernel(tc, context, D, z, conv_w, conv_b, t1, out):
+    nc = tc.nc
+    with ExitStack() as stack:
+        keep = stack.enter_context(tc.tile_pool(name="keep", bufs=1))
+        psum = stack.enter_context(tc.psum_pool(name="psum", bufs=8))
+        if PINNED:
+            stack.enter_context(tc.manual_schedule())
+
+        ident = keep.tile([P, P], F32)
+        make_identity(nc, ident[:])
+
+        z_sb = keep.tile([P, 4, 2, P], BF16)
+        d_sb = keep.tile([P, 4, M], BF16)
+        w_sb = keep.tile([P, 4, 2 * N], BF16)
+        c_sb = keep.tile([P, FRAMES + 1, N], BF16)
+        bias_bc = keep.tile([P, N], BF16)
+        t1_bf = keep.tile([P, 1], BF16)
+
+        for name in LOADS:
+            k = int(name[1:]) if len(name) > 1 else 0
+            if name == "z":
+                nc.sync.dma_start(out=z_sb[:], in_=z.rearrange("(u p e) b -> p u e b", u=4, e=2))
+            elif name == "t":
+                nc.sync.dma_start(out=t1_bf[:], in_=t1.partition_broadcast(P))
+            elif name == "b":
+                nc.sync.dma_start(out=bias_bc[:], in_=conv_b.partition_broadcast(P))
+            elif name[0] == "D":
+                nc.sync.dma_start(out=d_sb[:, k, :], in_=D[k * P:(k + 1) * P, :])
+            elif name[0] == "W":
+                nc.sync.dma_start(
+                    out=w_sb[:, k, :], in_=conv_w[k * P:(k + 1) * P].rearrange("o i t -> o (i t)")
+                )
+            else:
+                s0, s1 = C_GROUPS[k]
+                nc.sync.dma_start(
+                    out=c_sb[:, s0:s1, :], in_=context[s0:s1].rearrange("s b i -> b s i")
+                )
+
+        dT = keep.tile([P, 4 * N], F32)
+        dT_w = dT[:].rearrange("p (u i) -> p u i", u=4)
+        dT_bf = dT[:].bitcast(BF16).rearrange("p (u i e) -> p u i e", u=4, e=2)
+        zobs_sb = keep.tile([P, N], F32)
+        wg = keep.tile([P, 2, 4 * N], BF16, align_bytes=64)
+        wc = keep.tile([P, 2, N], U32, align_bytes=64)
+        ws = keep.tile([P, 2, N], U8, align_bytes=64)
+        wg_v = wg[:].rearrange("q t (o j) -> q t o j", j=4)
+        cg = keep.tile([P, (FRAMES + 1) * N], BF16, align_bytes=64)
+        cc = keep.tile([P, (FRAMES + 1) * P], U32, align_bytes=64)
+        cs = keep.tile([P, (FRAMES + 1) * P], U8, align_bytes=64)
+        diff = keep.tile([P, FRAMES, N], F32)
+        dist = keep.tile([P, FRAMES], F32)
+        junk = keep.tile([P, N], BF16)
+        rt1 = keep.tile([P, 1], F32)
+        dmin = keep.tile([P, 1], F32)
+        lg = keep.tile([P, FRAMES], F32)
+        ex = keep.tile([P, FRAMES], F32)
+        sume = keep.tile([P, 1], F32)
+        rs = keep.tile([P, 1], F32)
+        attn = keep.tile([P, FRAMES], F32)
+        acc_a = keep.tile([P, N], F32)
+        acc_b = keep.tile([P, N], F32)
+        acc_c = keep.tile([P, N], F32)
+        scaled = keep.tile([P, FRAMES, N], F32)
+        res = keep.tile([P, N], F32)
+        bank = {}
+        state = {"v_subs": 0, "v_ws": 0}
+
+        def copy_out(on_scalar, dst, src):
+            if on_scalar:
+                nc.scalar.copy(out=dst, in_=src)
+            else:
+                nc.vector.tensor_copy(out=dst, in_=src)
+
+        def td(c, h):
+            bank["D", c, h] = psum.tile([P, N], F32, tag="ps", name="ps_d%d%d" % (c, h))
+            words = d_sb[:, c, :].bitcast(F32)
+            for v in range(2):
+                u = 2 * h + v
+                nc.tensor.transpose(bank["D", c, h][:, v * P:(v + 1) * P], words[:, u * P:(u + 1) * P], ident[:])
+
+        def ed(c, h):
+            copy_out(
+                h == 1,
+                dT_w[:, 2 * h:2 * h + 2, c * P:(c + 1) * P],
+                bank["D", c, h][:, 0:2 * P].rearrange("p (u i) -> p u i", u=2),
+            )
+
+        def mz(c, h):
+            if c == 0:
+                bank["Z"] = psum.tile([P, N], F32, tag="ps", name="ps_z")
+            for k in range(8):
+                nc.tensor.matmul(
+                    bank["Z"][:, c * P:(c + 1) * P],
+                    lhsT=z_sb[:, k // 2, k % 2, :],
+                    rhs=dT_bf[:, k // 2, c * P:(c + 1) * P, k % 2],
+                    start=(k == 0),
+                    stop=(k == 7),
+                )
+
+        def tw(c, h):
+            bank["W", c] = psum.tile([P, N], F32, tag="ps", name="ps_w%d" % c)
+            words = w_sb[:, c, :].bitcast(F32).rearrange("o (u q e) -> o u e q", u=2, e=2)
+            for j in range(4):
+                nc.tensor.transpose(bank["W", c][:, j * P:(j + 1) * P], words[:, j // 2, j % 2, :], ident[:])
+
+        def ew(c, h):
+            copy_out(
+                c in EW_ON_SCALAR,
+                wg_v[:, :, c * P:(c + 1) * P, :],
+                bank["W", c][:].bitcast(BF16).rearrange("q (j o t) -> q t o j", j=4, t=2),
+            )
+
+        def qw(t, h):
+            nc.vector.quantize_mx(out=wc[:, t, :].bitcast(FP8X4), scales=ws[:, t, :], in_=wg[:, t, :])
+
+        def ez(a, h):
+            nc.scalar.copy(out=zobs_sb[:], in_=bank["Z"][:])
+
+        def tcx(g, h):
+            n = 2 if g < 8 else 1
+            bank["C", g] = psum.tile([P, N], F32, tag="ps", name="ps_c%d" % g)
+            for i in range(n):
+                words = c_sb[:, 2 * g + i, :].bitcast(F32)
+                for u in range(2):
+                    col = (2 * i + u) * P
+                    nc.tensor.transpose(bank["C", g][:, col:col + P], words[:, u * P:(u + 1) * P], ident[:])
+
+        def ec(g, h):
+            n = 2 if g < 8 else 1
+            copy_out(
+                g in EC_ON_SCALAR,
+                cg[:, 2 * g * N:(2 * g + n) * N].bitcast(F32).rearrange("q (s b u) -> q s b u", s=n, u=2),
+                bank["C", g][:, 0:2 * n * P].rearrange("q (s u b) -> q s b u", s=n, u=2),
+            )
+
+        def qc(g, h):
+            n = 2 if g < 8 else 1
+            nc.vector.quantize_mx(
+                out=cc[:, 2 * g * P:(2 * g + n) * P].bitcast(FP8X4),
+                scales=cs[:, 2 * g * P:(2 * g + n) * P],
+                in_=cg[:, 2 * g * N:(2 * g + n) * N],
+            )
+
+        def sub(s, h):
+            if s in SUB_ON_GPSIMD:
+                nc.gpsimd.tensor_tensor(out=diff[:, s, :], in0=c_sb[:, s, :], in1=zobs_sb[:], op=ALU.subtract)
+            else:
+                first = state["v_subs"] == 0 and len(SUB_ON_GPSIMD) > 0
+                state["v_subs"] = state["v_subs"] + 1
+                nc.vector.tensor_tensor(
+                    out=diff[:, s, :], in0=c_sb[:, s, :], in1=(zobs_sb[:] if first else bank["Z"][:]), op=ALU.subtract
+                )
+
+        def absum(s, h):
+            nc.scalar.activation(out=junk[:], in_=diff[:, s, :], func=ACT.Abs, accum_out=dist[:, s:s + 1])
+
+        def rt(a, h):
+            nc.vector.reciprocal(out=rt1[:], in_=t1_bf[:])
+
+        def sm(k, h):
+            if k == 1:
+                nc.vector.tensor_reduce(out=dmin[:], in_=dist[:], axis=AX.X, op=ALU.min)
+                nc.vector.tensor_scalar(
+                    out=lg[:], in0=dist[:], scalar1=dmin[:], scalar2=rt1[:], op0=ALU.subtract, op1=ALU.mult
+                )
+            elif k == 2:
+                nc.scalar.activation(out=ex[:], in_=lg[:], func=ACT.Exp, scale=-1.0, accum_out=sume[:])
+            else:
+                nc.vector.reciprocal(out=rs[:], in_=sume[:])
+                nc.vector.tensor_scalar(out=attn[:], in0=ex[:], scalar1=rs[:], scalar2=None, op0=ALU.mult)
+
+        def mx(s, h):
+            bank["X", s] = psum.tile([P, N], F32, tag="ps", name="ps_x%d" % s)
+            for t in range(2):
+                nc.tensor.matmul_mx(
+                    out=bank["X", s][:],
+                    lhsT=cc[:, (s + t) * P:(s + t + 1) * P].bitcast(FP8X4),
+                    lhsT_scale=cs[:, (s + t) * P:(s + t + 1) * P],
+                    rhs=wc[:, t, :].bitcast(FP8X4),
+                    rhs_scale=ws[:, t, :],
+                    start=(t == 0),
+                    stop=(t == 1),
+                )
+
+        def wsum(s, h):
+            enc = bank["X", s]
+            a_s = attn[:, s:s + 1]
+            if s in WS_ON_SCALAR:
+                nc.scalar.activation(out=scaled[:, s, :], in_=enc[:], func=ACT.Copy, scale=a_s)
+                return
+            k = state["v_ws"]
+            state["v_ws"] = k + 1
+            if k == 0:
+                nc.vector.scalar_tensor_tensor(
+                    out=acc_a[:], in0=enc[:], scalar=a_s, in1=bias_bc[:], op0=ALU.mult, op1=ALU.add
+                )
+            elif k == 1:
+                nc.vector.tensor_scalar(out=acc_b[:], in0=enc[:], scalar1=a_s, scalar2=None, op0=ALU.mult)
+            else:
+                acc = acc_a if k % 2 == 0 else acc_b
+                nc.vector.scalar_tensor_tensor(
+                    out=acc[:], in0=enc[:], scalar=a_s, in1=acc[:], op0=ALU.mult, op1=ALU.add
+                )
+
+        def ga(s, h):
+            k = WS_ON_SCALAR.index(s)
+            prev = scaled[:, WS_ON_SCALAR[0], :] if k == 1 else acc_c[:]
+            nc.gpsimd.tensor_tensor(out=acc_c[:], in0=prev, in1=scaled[:, s, :], op=ALU.add)
+
+        def mg(k, h):
+            last = len(WS_ON_SCALAR) == 0 or k == 2
+            dst = res if last else acc_a
+            if k == 1:
+                nc.vector.tensor_tensor(out=dst[:], in0=acc_a[:], in1=acc_b[:], op=ALU.add)
+            else:
+                nc.vector.tensor_tensor(out=dst[:], in0=acc_a[:], in1=acc_c[:], op=ALU.add)
+            if last:
+                nc.sync.dma_start(out=out[:, :], in_=res[:])
+
+        funcs = {
+            "TD": td, "ED": ed, "MZ": mz, "TW": tw, "EW": ew, "QW": qw, "EZ": ez, "TC": tcx, "EC": ec,
+            "QC": qc, "SUB": sub, "ABS": absum, "RT": rt, "SM": sm, "MX": mx, "WS": wsum, "GA": ga, "MG": mg,
+        }
+        for kind, a, h in ORDER:
+            funcs[kind](a, h)

@@ -18,37 +18,38 @@ N = 512
 M = 1024
 FLOPS = 2 * FRAMES * P * N * N * 2 + 2 * N * M * P
 
-EW_ON_SCALAR = (1, 3)
-EC_ON_SCALAR = (0, 6, 7, 8)
-SUB_ON_GPSIMD = (5, 6, 7, 8, 12, 14)
-WS_ON_SCALAR = (1, 4, 7, 8, 10)
+EW_ON_SCALAR = (0, 3)
+EC_ON_SCALAR = (0, 1, 2, 3, 7)
+SUB_ON_GPSIMD = (1, 8, 11, 15)
+WS_ON_SCALAR = (1, 4, 7, 10, 13)
 PINNED = True
 LOADS = ("z", "D0", "D1", "D2", "D3", "t", "W0", "W1", "W2", "W3", "c0", "c1", "c2", "c3", "c4", "b")
 C_GROUPS = ((0, 2), (2, 4), (4, 8), (8, 12), (12, 17))
 
 ORDER = (
     ("TD", 0, 0), ("TD", 0, 1), ("ED", 0, 0), ("ED", 0, 1), ("TD", 1, 0), ("TD", 1, 1),
-    ("ED", 1, 0), ("MZ", 0, 0), ("ED", 1, 1), ("TD", 2, 0), ("TD", 2, 1), ("ED", 2, 0),
-    ("TD", 3, 0), ("ED", 2, 1), ("TD", 3, 1), ("ED", 3, 0), ("MZ", 1, 0), ("ED", 3, 1),
-    ("TW", 0, 0), ("TW", 1, 0), ("EW", 0, 0), ("TW", 2, 0), ("EW", 1, 0), ("TW", 3, 0),
-    ("EW", 2, 0), ("MZ", 2, 0), ("EW", 3, 0), ("MZ", 3, 0), ("TC", 0, 0), ("EZ", 0, 0),
-    ("QW", 0, 0), ("RT", 0, 0), ("TC", 1, 0), ("EC", 0, 0), ("SUB", 0, 0), ("SUB", 5, 0),
-    ("TC", 2, 0), ("SUB", 1, 0), ("ABS", 0, 0), ("TC", 3, 0), ("SUB", 2, 0), ("ABS", 1, 0),
-    ("QW", 1, 0), ("SUB", 6, 0), ("ABS", 2, 0), ("TC", 4, 0), ("TC", 5, 0), ("SUB", 3, 0),
-    ("ABS", 5, 0), ("EC", 1, 0), ("SUB", 7, 0), ("ABS", 3, 0), ("SUB", 4, 0), ("ABS", 6, 0),
-    ("TC", 6, 0), ("EC", 2, 0), ("TC", 7, 0), ("SUB", 8, 0), ("ABS", 4, 0), ("TC", 8, 0),
-    ("QC", 0, 0), ("SUB", 9, 0), ("ABS", 7, 0), ("MX", 0, 0), ("SUB", 10, 0), ("ABS", 9, 0),
-    ("SUB", 12, 0), ("QC", 1, 0), ("ABS", 8, 0), ("SUB", 11, 0), ("ABS", 10, 0), ("SUB", 14, 0),
-    ("EC", 3, 0), ("ABS", 11, 0), ("QC", 2, 0), ("MX", 1, 0), ("SUB", 13, 0), ("ABS", 12, 0),
-    ("QC", 3, 0), ("ABS", 13, 0), ("SUB", 15, 0), ("ABS", 14, 0), ("EC", 4, 0), ("MX", 2, 0),
-    ("QC", 4, 0), ("ABS", 15, 0), ("MX", 3, 0), ("EC", 5, 0), ("EC", 6, 0), ("SM", 1, 0),
-    ("MX", 4, 0), ("QC", 5, 0), ("SM", 2, 0), ("QC", 6, 0), ("EC", 7, 0), ("MX", 5, 0),
-    ("SM", 3, 0), ("WS", 0, 0), ("EC", 8, 0), ("MX", 6, 0), ("WS", 1, 0), ("QC", 7, 0),
-    ("MX", 7, 0), ("QC", 8, 0), ("WS", 4, 0), ("WS", 2, 0), ("MX", 8, 0), ("WS", 7, 0),
-    ("GA", 4, 0), ("WS", 3, 0), ("MX", 9, 0), ("WS", 8, 0), ("WS", 5, 0), ("MX", 10, 0),
-    ("GA", 7, 0), ("WS", 6, 0), ("MX", 11, 0), ("WS", 10, 0), ("WS", 9, 0), ("MX", 12, 0),
-    ("MX", 13, 0), ("WS", 11, 0), ("GA", 8, 0), ("MX", 14, 0), ("WS", 12, 0), ("MX", 15, 0),
-    ("WS", 13, 0), ("GA", 10, 0), ("WS", 14, 0), ("WS", 15, 0), ("MG", 1, 0), ("MG", 2, 0),
+    ("MZ", 0, 0), ("ED", 1, 0), ("ED", 1, 1), ("TD", 2, 0), ("TD", 2, 1), ("TD", 3, 0),
+    ("ED", 2, 0), ("TD", 3, 1), ("ED", 2, 1), ("MZ", 1, 0), ("ED", 3, 0), ("GW", 0, 0),
+    ("ED", 3, 1), ("MZ", 2, 0), ("MZ", 3, 0), ("GW", 1, 0), ("TW", 0, 0), ("EZ", 0, 0),
+    ("EW", 0, 0), ("TC", 0, 0), ("SUB", 0, 0), ("SUB", 1, 0), ("TW", 1, 0), ("ABS", 0, 0),
+    ("SUB", 2, 0), ("EC", 0, 0), ("SUB", 3, 0), ("TC", 1, 0), ("GW", 2, 0), ("ABS", 1, 0),
+    ("EW", 1, 0), ("RT", 0, 0), ("TC", 2, 0), ("SUB", 4, 0), ("ABS", 2, 0), ("GW", 3, 0),
+    ("TC", 3, 0), ("SUB", 5, 0), ("ABS", 3, 0), ("TW", 2, 0), ("SUB", 6, 0), ("ABS", 4, 0),
+    ("SUB", 8, 0), ("SUB", 7, 0), ("TC", 4, 0), ("EC", 1, 0), ("EW", 2, 0), ("TC", 5, 0),
+    ("ABS", 5, 0), ("EC", 4, 0), ("SUB", 11, 0), ("ABS", 6, 0), ("TW", 3, 0), ("EC", 5, 0),
+    ("ABS", 7, 0), ("TC", 6, 0), ("SUB", 9, 0), ("SUB", 15, 0), ("EW", 3, 0), ("TC", 7, 0),
+    ("SUB", 10, 0), ("ABS", 8, 0), ("TC", 8, 0), ("EC", 6, 0), ("EC", 2, 0), ("QW", 0, 0),
+    ("ABS", 9, 0), ("QW", 1, 0), ("ABS", 10, 0), ("QC", 0, 0), ("QC", 1, 0), ("ABS", 11, 0),
+    ("MX", 0, 0), ("SUB", 12, 0), ("EC", 3, 0), ("MX", 1, 0), ("SUB", 13, 0), ("ABS", 12, 0),
+    ("MX", 2, 0), ("SUB", 14, 0), ("ABS", 13, 0), ("QC", 2, 0), ("QC", 3, 0), ("ABS", 14, 0),
+    ("MX", 3, 0), ("EC", 8, 0), ("QC", 4, 0), ("MX", 4, 0), ("ABS", 15, 0), ("QC", 5, 0),
+    ("QC", 6, 0), ("MX", 5, 0), ("EC", 7, 0), ("SM", 1, 0), ("QC", 8, 0), ("MX", 6, 0),
+    ("SM", 2, 0), ("QC", 7, 0), ("SM", 3, 0), ("MX", 7, 0), ("WS", 0, 0), ("WS", 1, 0),
+    ("WS", 2, 0), ("WS", 4, 0), ("MX", 8, 0), ("WS", 3, 0), ("WS", 7, 0), ("MX", 9, 0),
+    ("GA", 4, 0), ("WS", 5, 0), ("MX", 10, 0), ("MX", 11, 0), ("WS", 6, 0), ("WS", 10, 0),
+    ("GA", 7, 0), ("MX", 12, 0), ("WS", 8, 0), ("MX", 13, 0), ("WS", 9, 0), ("GA", 10, 0),
+    ("MX", 14, 0), ("WS", 11, 0), ("WS", 13, 0), ("MX", 15, 0), ("WS", 12, 0), ("GA", 13, 0),
+    ("WS", 14, 0), ("WS", 15, 0), ("MG", 1, 0), ("MG", 2, 0),
 )
 
 
@@ -97,7 +98,8 @@ def tile_dynamix_pa_kernel(tc, context, D, z, conv_w, conv_b, t1, out):
         wg = keep.tile([P, 2, 4 * N], BF16, align_bytes=64)
         wc = keep.tile([P, 2, N], U32, align_bytes=64)
         ws = keep.tile([P, 2, N], U8, align_bytes=64)
-        wg_v = wg[:].rearrange("q t (o j) -> q t o j", j=4)
+        wg_w = wg[:].rearrange("q t k -> q (t k)").bitcast(F32).rearrange("q (t o u) -> q t o u", t=2, u=2)
+        w_taps = keep.tile([P, 4, 2, N], BF16)
         cg = keep.tile([P, (FRAMES + 1) * N], BF16, align_bytes=64)
         cc = keep.tile([P, (FRAMES + 1) * P], U32, align_bytes=64)
         cs = keep.tile([P, (FRAMES + 1) * P], U8, align_bytes=64)
@@ -151,17 +153,28 @@ def tile_dynamix_pa_kernel(tc, context, D, z, conv_w, conv_b, t1, out):
                     stop=(k == 7),
                 )
 
+        def gw(c, h):
+            nc.gpsimd.tensor_scalar(
+                out=w_taps[:, c, :, :],
+                in0=w_sb[:, c, :].rearrange("o (i t) -> o t i", t=2),
+                scalar1=1.0,
+                scalar2=0.0,
+                op0=ALU.mult,
+                op1=ALU.add,
+            )
+
         def tw(c, h):
             bank["W", c] = psum.tile([P, N], F32, tag="ps", name="ps_w%d" % c)
-            words = w_sb[:, c, :].bitcast(F32).rearrange("o (u q e) -> o u e q", u=2, e=2)
             for j in range(4):
-                nc.tensor.transpose(bank["W", c][:, j * P:(j + 1) * P], words[:, j // 2, j % 2, :], ident[:])
+                words = w_taps[:, c, j // 2, :].bitcast(F32)
+                u = j % 2
+                nc.tensor.transpose(bank["W", c][:, j * P:(j + 1) * P], words[:, u * P:(u + 1) * P], ident[:])
 
         def ew(c, h):
             copy_out(
                 c in EW_ON_SCALAR,
-                wg_v[:, :, c * P:(c + 1) * P, :],
-                bank["W", c][:].bitcast(BF16).rearrange("q (j o t) -> q t o j", j=4, t=2),
+                wg_w[:, :, c * P:(c + 1) * P, :],
+                bank["W", c][:].rearrange("q (t u o) -> q t o u", t=2, u=2),
             )
 
         def qw(t, h):
@@ -272,7 +285,7 @@ def tile_dynamix_pa_kernel(tc, context, D, z, conv_w, conv_b, t1, out):
                 nc.sync.dma_start(out=out[:, :], in_=res[:])
 
         funcs = {
-            "TD": td, "ED": ed, "MZ": mz, "TW": tw, "EW": ew, "QW": qw, "EZ": ez, "TC": tcx, "EC": ec,
+            "GW": gw, "TD": td, "ED": ed, "MZ": mz, "TW": tw, "EW": ew, "QW": qw, "EZ": ez, "TC": tcx, "EC": ec,
             "QC": qc, "SUB": sub, "ABS": absum, "RT": rt, "SM": sm, "MX": mx, "WS": wsum, "GA": ga, "MG": mg,
         }
         for kind, a, h in ORDER:

@@ -18,38 +18,38 @@ N = 512
 M = 1024
 FLOPS = 2 * FRAMES * P * N * N * 2 + 2 * N * M * P
 
-EW_ON_SCALAR = (0, 3)
-EC_ON_SCALAR = (0, 1, 2, 3, 7)
-SUB_ON_GPSIMD = (1, 8, 11, 15)
-WS_ON_SCALAR = (1, 4, 7, 10, 13)
+EW_ON_SCALAR = (3,)
+EC_ON_SCALAR = (0, 1, 2, 3, 7, 8)
+SUB_ON_GPSIMD = (1, 2, 8, 15)
+WS_ON_SCALAR = (2, 4, 5, 7, 12)
 PINNED = True
-LOADS = ("z", "D0", "D1", "D2", "D3", "t", "W0", "W1", "W2", "W3", "c0", "c1", "c2", "c3", "c4", "b")
-C_GROUPS = ((0, 2), (2, 4), (4, 8), (8, 12), (12, 17))
+LOADS = ("D0", "D1", "z", "D2", "D3", "t", "W0", "W1", "W2", "W3", "c0", "c1", "c2", "c3", "c4", "c5", "c6", "c7", "c8", "b")
+C_GROUPS = ((0, 2), (2, 4), (4, 6), (6, 8), (8, 10), (10, 12), (12, 14), (14, 16), (16, 17))
 
 ORDER = (
-    ("TD", 0, 0), ("TD", 0, 1), ("ED", 0, 0), ("ED", 0, 1), ("TD", 1, 0), ("TD", 1, 1),
-    ("MZ", 0, 0), ("ED", 1, 0), ("ED", 1, 1), ("TD", 2, 0), ("TD", 2, 1), ("TD", 3, 0),
-    ("ED", 2, 0), ("TD", 3, 1), ("ED", 2, 1), ("MZ", 1, 0), ("ED", 3, 0), ("GW", 0, 0),
-    ("ED", 3, 1), ("MZ", 2, 0), ("MZ", 3, 0), ("GW", 1, 0), ("TW", 0, 0), ("EZ", 0, 0),
-    ("EW", 0, 0), ("TC", 0, 0), ("SUB", 0, 0), ("SUB", 1, 0), ("TW", 1, 0), ("ABS", 0, 0),
-    ("SUB", 2, 0), ("EC", 0, 0), ("SUB", 3, 0), ("TC", 1, 0), ("GW", 2, 0), ("ABS", 1, 0),
-    ("EW", 1, 0), ("RT", 0, 0), ("TC", 2, 0), ("SUB", 4, 0), ("ABS", 2, 0), ("GW", 3, 0),
-    ("TC", 3, 0), ("SUB", 5, 0), ("ABS", 3, 0), ("TW", 2, 0), ("SUB", 6, 0), ("ABS", 4, 0),
-    ("SUB", 8, 0), ("SUB", 7, 0), ("TC", 4, 0), ("EC", 1, 0), ("EW", 2, 0), ("TC", 5, 0),
-    ("ABS", 5, 0), ("EC", 4, 0), ("SUB", 11, 0), ("ABS", 6, 0), ("TW", 3, 0), ("EC", 5, 0),
-    ("ABS", 7, 0), ("TC", 6, 0), ("SUB", 9, 0), ("SUB", 15, 0), ("EW", 3, 0), ("TC", 7, 0),
-    ("SUB", 10, 0), ("ABS", 8, 0), ("TC", 8, 0), ("EC", 6, 0), ("EC", 2, 0), ("QW", 0, 0),
-    ("ABS", 9, 0), ("QW", 1, 0), ("ABS", 10, 0), ("QC", 0, 0), ("QC", 1, 0), ("ABS", 11, 0),
-    ("MX", 0, 0), ("SUB", 12, 0), ("EC", 3, 0), ("MX", 1, 0), ("SUB", 13, 0), ("ABS", 12, 0),
-    ("MX", 2, 0), ("SUB", 14, 0), ("ABS", 13, 0), ("QC", 2, 0), ("QC", 3, 0), ("ABS", 14, 0),
-    ("MX", 3, 0), ("EC", 8, 0), ("QC", 4, 0), ("MX", 4, 0), ("ABS", 15, 0), ("QC", 5, 0),
-    ("QC", 6, 0), ("MX", 5, 0), ("EC", 7, 0), ("SM", 1, 0), ("QC", 8, 0), ("MX", 6, 0),
-    ("SM", 2, 0), ("QC", 7, 0), ("SM", 3, 0), ("MX", 7, 0), ("WS", 0, 0), ("WS", 1, 0),
-    ("WS", 2, 0), ("WS", 4, 0), ("MX", 8, 0), ("WS", 3, 0), ("WS", 7, 0), ("MX", 9, 0),
-    ("GA", 4, 0), ("WS", 5, 0), ("MX", 10, 0), ("MX", 11, 0), ("WS", 6, 0), ("WS", 10, 0),
-    ("GA", 7, 0), ("MX", 12, 0), ("WS", 8, 0), ("MX", 13, 0), ("WS", 9, 0), ("GA", 10, 0),
-    ("MX", 14, 0), ("WS", 11, 0), ("WS", 13, 0), ("MX", 15, 0), ("WS", 12, 0), ("GA", 13, 0),
-    ("WS", 14, 0), ("WS", 15, 0), ("MG", 1, 0), ("MG", 2, 0),
+    ("WM", 5, 0), ("TD", 0, 0), ("TD", 0, 1), ("ED", 0, 0), ("TD", 1, 0), ("ED", 0, 1),
+    ("TD", 1, 1), ("ED", 1, 0), ("ED", 1, 1), ("MZ", 0, 0), ("MZ", 1, 0), ("TD", 2, 0),
+    ("TD", 2, 1), ("TD", 3, 0), ("TD", 3, 1), ("ED", 2, 0), ("ED", 2, 1), ("GW", 0, 0),
+    ("ED", 3, 0), ("ED", 3, 1), ("MZ", 2, 0), ("MZ", 3, 0), ("GW", 1, 0), ("TW", 0, 0),
+    ("EZ", 0, 0), ("GW", 2, 0), ("TC", 0, 0), ("EW", 0, 0), ("SUB", 0, 0), ("TW", 1, 0),
+    ("EC", 0, 0), ("SUB", 3, 0), ("SUB", 1, 0), ("TC", 1, 0), ("ABS", 0, 0), ("EW", 1, 0),
+    ("RT", 0, 0), ("TW", 2, 0), ("ABS", 3, 0), ("SUB", 4, 0), ("SUB", 2, 0), ("TC", 2, 0),
+    ("EC", 1, 0), ("SUB", 5, 0), ("TC", 3, 0), ("ABS", 1, 0), ("EW", 2, 0), ("GW", 3, 0),
+    ("TC", 4, 0), ("ABS", 4, 0), ("SUB", 6, 0), ("ABS", 2, 0), ("SUB", 7, 0), ("TC", 5, 0),
+    ("SUB", 8, 0), ("SUB", 9, 0), ("ABS", 5, 0), ("TC", 6, 0), ("SUB", 10, 0), ("ABS", 6, 0),
+    ("TW", 3, 0), ("SUB", 11, 0), ("ABS", 7, 0), ("SUB", 15, 0), ("TC", 7, 0), ("SUB", 12, 0),
+    ("EW", 3, 0), ("SUB", 13, 0), ("ABS", 8, 0), ("TC", 8, 0), ("QC", 0, 0), ("ABS", 9, 0),
+    ("QC", 1, 0), ("QW", 0, 0), ("ABS", 10, 0), ("QW", 1, 0), ("ABS", 11, 0), ("SUB", 14, 0),
+    ("ABS", 12, 0), ("EC", 4, 0), ("ABS", 13, 0), ("MX", 0, 0), ("QC", 4, 0), ("ABS", 14, 0),
+    ("EC", 5, 0), ("MX", 1, 0), ("QC", 5, 0), ("ABS", 15, 0), ("EC", 6, 0), ("MX", 2, 0),
+    ("EC", 2, 0), ("QC", 6, 0), ("SM", 1, 0), ("EC", 3, 0), ("MX", 8, 0), ("QC", 2, 0),
+    ("SM", 2, 0), ("MX", 9, 0), ("EC", 7, 0), ("QC", 3, 0), ("MX", 3, 0), ("SM", 3, 0),
+    ("EC", 8, 0), ("WS", 0, 0), ("MX", 4, 0), ("WS", 2, 0), ("QC", 7, 0), ("MX", 5, 0),
+    ("QC", 8, 0), ("WS", 1, 0), ("WS", 4, 0), ("MX", 6, 0), ("WS", 3, 0), ("WS", 5, 0),
+    ("MX", 7, 0), ("GA", 4, 0), ("WS", 8, 0), ("MX", 10, 0), ("WS", 7, 0), ("WS", 6, 0),
+    ("MX", 11, 0), ("GA", 5, 0), ("WS", 9, 0), ("MX", 12, 0), ("WS", 10, 0), ("MX", 13, 0),
+    ("WS", 12, 0), ("GA", 7, 0), ("WS", 11, 0), ("MX", 14, 0), ("MX", 15, 0), ("WS", 13, 0),
+    ("GA", 12, 0), ("WS", 14, 0), ("WS", 15, 0), ("MG", 1, 0), ("MG", 2, 0),
 )
 
 
@@ -126,6 +126,11 @@ def tile_dynamix_pa_kernel(tc, context, D, z, conv_w, conv_b, t1, out):
                 nc.scalar.copy(out=dst, in_=src)
             else:
                 nc.vector.tensor_copy(out=dst, in_=src)
+
+        def wm(n, h):
+            bank["M"] = psum.tile([P, N], F32, tag="ps", name="ps_m")
+            for k in range(n):
+                nc.tensor.matmul(bank["M"][:, 0:P], lhsT=ident[:], rhs=ident[:], start=True, stop=True)
 
         def td(c, h):
             bank["D", c, h] = psum.tile([P, N], F32, tag="ps", name="ps_d%d%d" % (c, h))
@@ -285,7 +290,7 @@ def tile_dynamix_pa_kernel(tc, context, D, z, conv_w, conv_b, t1, out):
                 nc.sync.dma_start(out=out[:, :], in_=res[:])
 
         funcs = {
-            "GW": gw, "TD": td, "ED": ed, "MZ": mz, "TW": tw, "EW": ew, "QW": qw, "EZ": ez, "TC": tcx, "EC": ec,
+            "WM": wm, "GW": gw, "TD": td, "ED": ed, "MZ": mz, "TW": tw, "EW": ew, "QW": qw, "EZ": ez, "TC": tcx, "EC": ec,
             "QC": qc, "SUB": sub, "ABS": absum, "RT": rt, "SM": sm, "MX": mx, "WS": wsum, "GA": ga, "MG": mg,
         }
         for kind, a, h in ORDER:

@@ -14,151 +14,115 @@ AX = mybir.AxisListType
 
 P = 128
 FRAMES = 16
-N = 512
-M = 1024
-FLOPS = 2 * FRAMES * P * N * N * 2 + 2 * N * M * P
+LOADED = FRAMES + 1
+CH = 512
+LATENT = 1024
+PAIRS = LOADED // 2
+PSUM_BANKS = 8
+FLOPS = 2 * FRAMES * P * CH * CH * 2 + 2 * CH * LATENT * P
 
-EW_ON_SCALAR = (3,)
-EC_ON_SCALAR = (0, 1, 2, 3, 7, 8)
-SUB_ON_GPSIMD = (1, 2, 8, 15)
-WS_ON_SCALAR = (2, 4, 5, 7, 12)
-PINNED = True
-LOADS = ("D0", "D1", "z", "D2", "D3", "t", "W0", "W1", "W2", "W3", "c0", "c1", "c2", "c3", "c4", "c5", "c6", "c7", "c8", "b")
-C_GROUPS = ((0, 2), (2, 4), (4, 6), (6, 8), (8, 10), (10, 12), (12, 14), (14, 16), (16, 17))
-
-ORDER = (
-    ("WM", 5, 0), ("TD", 0, 0), ("TD", 0, 1), ("ED", 0, 0), ("TD", 1, 0), ("ED", 0, 1),
-    ("TD", 1, 1), ("ED", 1, 0), ("ED", 1, 1), ("MZ", 0, 0), ("MZ", 1, 0), ("TD", 2, 0),
-    ("TD", 2, 1), ("TD", 3, 0), ("TD", 3, 1), ("ED", 2, 0), ("ED", 2, 1), ("GW", 0, 0),
-    ("ED", 3, 0), ("ED", 3, 1), ("MZ", 2, 0), ("MZ", 3, 0), ("GW", 1, 0), ("TW", 0, 0),
-    ("EZ", 0, 0), ("GW", 2, 0), ("TC", 0, 0), ("EW", 0, 0), ("SUB", 0, 0), ("TW", 1, 0),
-    ("EC", 0, 0), ("SUB", 3, 0), ("SUB", 1, 0), ("TC", 1, 0), ("ABS", 0, 0), ("EW", 1, 0),
-    ("RT", 0, 0), ("TW", 2, 0), ("ABS", 3, 0), ("SUB", 4, 0), ("SUB", 2, 0), ("TC", 2, 0),
-    ("EC", 1, 0), ("SUB", 5, 0), ("TC", 3, 0), ("ABS", 1, 0), ("EW", 2, 0), ("GW", 3, 0),
-    ("TC", 4, 0), ("ABS", 4, 0), ("SUB", 6, 0), ("ABS", 2, 0), ("SUB", 7, 0), ("TC", 5, 0),
-    ("SUB", 8, 0), ("SUB", 9, 0), ("ABS", 5, 0), ("TC", 6, 0), ("SUB", 10, 0), ("ABS", 6, 0),
-    ("TW", 3, 0), ("SUB", 11, 0), ("ABS", 7, 0), ("SUB", 15, 0), ("TC", 7, 0), ("SUB", 12, 0),
-    ("EW", 3, 0), ("SUB", 13, 0), ("ABS", 8, 0), ("TC", 8, 0), ("QC", 0, 0), ("ABS", 9, 0),
-    ("QC", 1, 0), ("QW", 0, 0), ("ABS", 10, 0), ("QW", 1, 0), ("ABS", 11, 0), ("SUB", 14, 0),
-    ("ABS", 12, 0), ("EC", 4, 0), ("ABS", 13, 0), ("MX", 0, 0), ("QC", 4, 0), ("ABS", 14, 0),
-    ("EC", 5, 0), ("MX", 1, 0), ("QC", 5, 0), ("ABS", 15, 0), ("EC", 6, 0), ("MX", 2, 0),
-    ("EC", 2, 0), ("QC", 6, 0), ("SM", 1, 0), ("EC", 3, 0), ("MX", 8, 0), ("QC", 2, 0),
-    ("SM", 2, 0), ("MX", 9, 0), ("EC", 7, 0), ("QC", 3, 0), ("MX", 3, 0), ("SM", 3, 0),
-    ("EC", 8, 0), ("WS", 0, 0), ("MX", 4, 0), ("WS", 2, 0), ("QC", 7, 0), ("MX", 5, 0),
-    ("QC", 8, 0), ("WS", 1, 0), ("WS", 4, 0), ("MX", 6, 0), ("WS", 3, 0), ("WS", 5, 0),
-    ("MX", 7, 0), ("GA", 4, 0), ("WS", 8, 0), ("MX", 10, 0), ("WS", 7, 0), ("WS", 6, 0),
-    ("MX", 11, 0), ("GA", 5, 0), ("WS", 9, 0), ("MX", 12, 0), ("WS", 10, 0), ("MX", 13, 0),
-    ("WS", 12, 0), ("GA", 7, 0), ("WS", 11, 0), ("MX", 14, 0), ("MX", 15, 0), ("WS", 13, 0),
-    ("GA", 12, 0), ("WS", 14, 0), ("WS", 15, 0), ("MG", 1, 0), ("MG", 2, 0),
+GPSIMD_PAIRS = (6, 7)
+SCALAR_FRAMES = (1, 4, 7, 10, 13)
+VECTOR_FRAMES = tuple(s for s in range(FRAMES) if s not in SCALAR_FRAMES)
+BANK_STEPS = (
+    (("C", 0), ("C", 1)),
+    (("W", 0), ("C", 2)),
+    (("W", 1), ("C", 3)),
+    (("W", 2), ("C", 4)),
+    (("W", 3), ("C", 5)),
+    (("C", 6), ("C", 7)),
+    (("C", 8),),
 )
+AHEAD = 2
 
 
 def tile_dynamix_pa_kernel(tc, context, D, z, conv_w, conv_b, t1, out):
     nc = tc.nc
     with ExitStack() as stack:
         keep = stack.enter_context(tc.tile_pool(name="keep", bufs=1))
-        psum = stack.enter_context(tc.psum_pool(name="psum", bufs=8))
-        if PINNED:
-            stack.enter_context(tc.manual_schedule())
+        psum = stack.enter_context(tc.psum_pool(name="psum", bufs=PSUM_BANKS))
+        stack.enter_context(tc.manual_schedule())
 
         ident = keep.tile([P, P], F32)
         make_identity(nc, ident[:])
 
+        d_sb = keep.tile([P, 4, LATENT], BF16)
         z_sb = keep.tile([P, 4, 2, P], BF16)
-        d_sb = keep.tile([P, 4, M], BF16)
-        w_sb = keep.tile([P, 4, 2 * N], BF16)
-        c_sb = keep.tile([P, FRAMES + 1, N], BF16)
-        bias_bc = keep.tile([P, N], BF16)
         t1_bf = keep.tile([P, 1], BF16)
+        c_sb = keep.tile([P, LOADED, CH], BF16)
+        w_sb = keep.tile([P, 4, 2 * CH], BF16)
+        bias_bc = keep.tile([P, CH], BF16)
 
-        for name in LOADS:
-            k = int(name[1:]) if len(name) > 1 else 0
-            if name == "z":
-                nc.sync.dma_start(out=z_sb[:], in_=z.rearrange("(u p e) b -> p u e b", u=4, e=2))
-            elif name == "t":
-                nc.sync.dma_start(out=t1_bf[:], in_=t1.partition_broadcast(P))
-            elif name == "b":
-                nc.sync.dma_start(out=bias_bc[:], in_=conv_b.partition_broadcast(P))
-            elif name[0] == "D":
-                nc.sync.dma_start(out=d_sb[:, k, :], in_=D[k * P:(k + 1) * P, :])
-            elif name[0] == "W":
-                nc.sync.dma_start(
-                    out=w_sb[:, k, :], in_=conv_w[k * P:(k + 1) * P].rearrange("o i t -> o (i t)")
-                )
-            else:
-                s0, s1 = C_GROUPS[k]
-                nc.sync.dma_start(
-                    out=c_sb[:, s0:s1, :], in_=context[s0:s1].rearrange("s b i -> b s i")
-                )
+        def load_d(c):
+            nc.sync.dma_start(out=d_sb[:, c, :], in_=D[c * P:(c + 1) * P, :])
 
-        dT = keep.tile([P, 4 * N], F32)
-        dT_w = dT[:].rearrange("p (u i) -> p u i", u=4)
-        dT_bf = dT[:].bitcast(BF16).rearrange("p (u i e) -> p u i e", u=4, e=2)
-        zobs_sb = keep.tile([P, N], F32)
-        wg = keep.tile([P, 2, 4 * N], BF16, align_bytes=64)
-        wc = keep.tile([P, 2, N], U32, align_bytes=64)
-        ws = keep.tile([P, 2, N], U8, align_bytes=64)
-        wg_w = wg[:].rearrange("q t k -> q (t k)").bitcast(F32).rearrange("q (t o u) -> q t o u", t=2, u=2)
-        w_taps = keep.tile([P, 4, 2, N], BF16)
-        cg = keep.tile([P, (FRAMES + 1) * N], BF16, align_bytes=64)
-        cc = keep.tile([P, (FRAMES + 1) * P], U32, align_bytes=64)
-        cs = keep.tile([P, (FRAMES + 1) * P], U8, align_bytes=64)
-        diff = keep.tile([P, FRAMES, N], F32)
-        dist = keep.tile([P, FRAMES], F32)
-        junk = keep.tile([P, N], BF16)
-        rt1 = keep.tile([P, 1], F32)
-        dmin = keep.tile([P, 1], F32)
-        lg = keep.tile([P, FRAMES], F32)
-        ex = keep.tile([P, FRAMES], F32)
-        sume = keep.tile([P, 1], F32)
-        rs = keep.tile([P, 1], F32)
-        attn = keep.tile([P, FRAMES], F32)
-        acc_a = keep.tile([P, N], F32)
-        acc_b = keep.tile([P, N], F32)
-        acc_c = keep.tile([P, N], F32)
-        scaled = keep.tile([P, FRAMES, N], F32)
-        res = keep.tile([P, N], F32)
+        def load_frames(g):
+            s0, s1 = 2 * g, min(2 * g + 2, LOADED)
+            nc.sync.dma_start(out=c_sb[:, s0:s1, :], in_=context[s0:s1].rearrange("s b i -> b s i"))
+
+        load_d(0)
+        load_d(1)
+        nc.sync.dma_start(out=z_sb[:], in_=z.rearrange("(u q e) b -> q u e b", u=4, e=2))
+        load_d(2)
+        load_d(3)
+        nc.sync.dma_start(out=t1_bf[:], in_=t1.partition_broadcast(P))
+        load_frames(0)
+        load_frames(1)
+        for c in range(4):
+            nc.sync.dma_start(out=w_sb[:, c, :], in_=conv_w[c * P:(c + 1) * P].rearrange("o i t -> o (i t)"))
+        for g in range(2, PAIRS + 1):
+            load_frames(g)
+        nc.sync.dma_start(out=bias_bc[:], in_=conv_b.partition_broadcast(P))
+
         bank = {}
-        state = {"v_subs": 0, "v_ws": 0}
 
-        def copy_out(on_scalar, dst, src):
-            if on_scalar:
-                nc.scalar.copy(out=dst, in_=src)
-            else:
-                nc.vector.tensor_copy(out=dst, in_=src)
+        def new_bank(key, name):
+            bank[key] = psum.tile([P, CH], F32, tag="bank", name=name)
+            return bank[key]
 
-        def wm(n, h):
-            bank["M"] = psum.tile([P, N], F32, tag="ps", name="ps_m")
-            for k in range(n):
-                nc.tensor.matmul(bank["M"][:, 0:P], lhsT=ident[:], rhs=ident[:], start=True, stop=True)
+        d_t = keep.tile([P, 4 * CH], F32)
+        d_t_words = d_t[:].rearrange("q (u i) -> q u i", u=4)
+        d_t_halves = d_t[:].bitcast(BF16).rearrange("q (u i e) -> q u i e", u=4, e=2)
 
-        def td(c, h):
-            bank["D", c, h] = psum.tile([P, N], F32, tag="ps", name="ps_d%d%d" % (c, h))
+        def transpose_d(c):
             words = d_sb[:, c, :].bitcast(F32)
-            for v in range(2):
-                u = 2 * h + v
-                nc.tensor.transpose(bank["D", c, h][:, v * P:(v + 1) * P], words[:, u * P:(u + 1) * P], ident[:])
+            for h in range(2):
+                target = new_bank(("D", c, h), "d%d%d" % (c, h))
+                for v in range(2):
+                    u = 2 * h + v
+                    nc.tensor.transpose(target[:, v * P:(v + 1) * P], words[:, u * P:(u + 1) * P], ident[:])
 
-        def ed(c, h):
-            copy_out(
-                h == 1,
-                dT_w[:, 2 * h:2 * h + 2, c * P:(c + 1) * P],
-                bank["D", c, h][:, 0:2 * P].rearrange("p (u i) -> p u i", u=2),
+        def copy_d(c):
+            cols = slice(c * P, (c + 1) * P)
+            nc.vector.tensor_copy(
+                out=d_t_words[:, 0:2, cols], in_=bank["D", c, 0][:, 0:2 * P].rearrange("q (u i) -> q u i", u=2)
+            )
+            nc.scalar.copy(
+                out=d_t_words[:, 2:4, cols], in_=bank["D", c, 1][:, 0:2 * P].rearrange("q (u i) -> q u i", u=2)
             )
 
-        def mz(c, h):
-            if c == 0:
-                bank["Z"] = psum.tile([P, N], F32, tag="ps", name="ps_z")
+        def z_obs_columns(c):
+            cols = slice(c * P, (c + 1) * P)
             for k in range(8):
                 nc.tensor.matmul(
-                    bank["Z"][:, c * P:(c + 1) * P],
+                    bank["Z"][:, cols],
                     lhsT=z_sb[:, k // 2, k % 2, :],
-                    rhs=dT_bf[:, k // 2, c * P:(c + 1) * P, k % 2],
+                    rhs=d_t_halves[:, k // 2, cols, k % 2],
                     start=(k == 0),
                     stop=(k == 7),
                 )
 
-        def gw(c, h):
+        for c in range(4):
+            transpose_d(c)
+            copy_d(c)
+            if c == 1:
+                new_bank("Z", "z_obs")
+            if c > 0:
+                z_obs_columns(c - 1)
+        z_obs_columns(3)
+
+        w_taps = keep.tile([P, 4, 2, CH], BF16)
+        for c in range(4):
             nc.gpsimd.tensor_scalar(
                 out=w_taps[:, c, :, :],
                 in0=w_sb[:, c, :].rearrange("o (i t) -> o t i", t=2),
@@ -168,130 +132,154 @@ def tile_dynamix_pa_kernel(tc, context, D, z, conv_w, conv_b, t1, out):
                 op1=ALU.add,
             )
 
-        def tw(c, h):
-            bank["W", c] = psum.tile([P, N], F32, tag="ps", name="ps_w%d" % c)
-            for j in range(4):
-                words = w_taps[:, c, j // 2, :].bitcast(F32)
-                u = j % 2
-                nc.tensor.transpose(bank["W", c][:, j * P:(j + 1) * P], words[:, u * P:(u + 1) * P], ident[:])
+        c_grouped = keep.tile([P, LOADED * CH], BF16, align_bytes=64)
+        c_codes = keep.tile([P, LOADED * P], U32, align_bytes=64)
+        c_scales = keep.tile([P, LOADED * P], U8, align_bytes=64)
+        w_grouped = keep.tile([P, 2, 4 * CH], BF16, align_bytes=64)
+        w_codes = keep.tile([P, 2, CH], U32, align_bytes=64)
+        w_scales = keep.tile([P, 2, CH], U8, align_bytes=64)
+        w_grouped_words = (
+            w_grouped[:].rearrange("q t k -> q (t k)").bitcast(F32).rearrange("q (t o u) -> q t o u", t=2, u=2)
+        )
 
-        def ew(c, h):
-            copy_out(
-                c in EW_ON_SCALAR,
-                wg_w[:, :, c * P:(c + 1) * P, :],
-                bank["W", c][:].rearrange("q (t u o) -> q t o u", t=2, u=2),
-            )
+        def frames_of(g):
+            return min(2, LOADED - 2 * g)
 
-        def qw(t, h):
-            nc.vector.quantize_mx(out=wc[:, t, :].bitcast(FP8X4), scales=ws[:, t, :], in_=wg[:, t, :])
+        def transpose_bank(kind, j):
+            target = new_bank((kind, j), "%s%d" % (kind, j))
+            for v in range(4 if kind == "W" else 2 * frames_of(j)):
+                row = w_taps[:, j, v // 2, :] if kind == "W" else c_sb[:, 2 * j + v // 2, :]
+                u = v % 2
+                nc.tensor.transpose(target[:, v * P:(v + 1) * P], row.bitcast(F32)[:, u * P:(u + 1) * P], ident[:])
 
-        def ez(a, h):
-            nc.scalar.copy(out=zobs_sb[:], in_=bank["Z"][:])
-
-        def tcx(g, h):
-            n = 2 if g < 8 else 1
-            bank["C", g] = psum.tile([P, N], F32, tag="ps", name="ps_c%d" % g)
-            for i in range(n):
-                words = c_sb[:, 2 * g + i, :].bitcast(F32)
-                for u in range(2):
-                    col = (2 * i + u) * P
-                    nc.tensor.transpose(bank["C", g][:, col:col + P], words[:, u * P:(u + 1) * P], ident[:])
-
-        def ec(g, h):
-            n = 2 if g < 8 else 1
-            copy_out(
-                g in EC_ON_SCALAR,
-                cg[:, 2 * g * N:(2 * g + n) * N].bitcast(F32).rearrange("q (s b u) -> q s b u", s=n, u=2),
-                bank["C", g][:, 0:2 * n * P].rearrange("q (s u b) -> q s b u", s=n, u=2),
-            )
-
-        def qc(g, h):
-            n = 2 if g < 8 else 1
-            nc.vector.quantize_mx(
-                out=cc[:, 2 * g * P:(2 * g + n) * P].bitcast(FP8X4),
-                scales=cs[:, 2 * g * P:(2 * g + n) * P],
-                in_=cg[:, 2 * g * N:(2 * g + n) * N],
-            )
-
-        def sub(s, h):
-            if s in SUB_ON_GPSIMD:
-                nc.gpsimd.tensor_tensor(out=diff[:, s, :], in0=c_sb[:, s, :], in1=zobs_sb[:], op=ALU.subtract)
+        def empty_bank(kind, j, on_scalar):
+            if kind == "W":
+                dst = w_grouped_words[:, :, j * P:(j + 1) * P, :]
+                src = bank[kind, j][:].rearrange("q (t u o) -> q t o u", t=2, u=2)
             else:
-                first = state["v_subs"] == 0 and len(SUB_ON_GPSIMD) > 0
-                state["v_subs"] = state["v_subs"] + 1
+                n = frames_of(j)
+                dst = c_grouped[:, 2 * j * CH:(2 * j + n) * CH].bitcast(F32).rearrange(
+                    "q (s b u) -> q s b u", s=n, u=2
+                )
+                src = bank[kind, j][:, 0:2 * n * P].rearrange("q (s u b) -> q s b u", s=n, u=2)
+            if on_scalar:
+                nc.scalar.copy(out=dst, in_=src)
+            else:
+                nc.vector.tensor_copy(out=dst, in_=src)
+
+        z_obs_sb = keep.tile([P, CH], F32)
+        diff = keep.tile([P, FRAMES, CH], F32)
+        dist = keep.tile([P, FRAMES], F32)
+        unused = keep.tile([P, CH], BF16)
+        inv_t1 = keep.tile([P, 1], F32)
+
+        for step in BANK_STEPS[0:AHEAD]:
+            for kind, j in step:
+                transpose_bank(kind, j)
+        for k in range(PAIRS):
+            step = BANK_STEPS[k] if k < len(BANK_STEPS) else ()
+            if len(step) > 0:
+                empty_bank(step[0][0], step[0][1], True)
+            if k not in GPSIMD_PAIRS:
                 nc.vector.tensor_tensor(
-                    out=diff[:, s, :], in0=c_sb[:, s, :], in1=(zobs_sb[:] if first else bank["Z"][:]), op=ALU.subtract
+                    out=diff[:, 2 * k:2 * k + 2, :],
+                    in0=c_sb[:, 2 * k:2 * k + 2, :],
+                    in1=bank["Z"][:].unsqueeze(1).to_broadcast([P, 2, CH]),
+                    op=ALU.subtract,
                 )
-
-        def absum(s, h):
-            nc.scalar.activation(out=junk[:], in_=diff[:, s, :], func=ACT.Abs, accum_out=dist[:, s:s + 1])
-
-        def rt(a, h):
-            nc.vector.reciprocal(out=rt1[:], in_=t1_bf[:])
-
-        def sm(k, h):
+            for s in (2 * k, 2 * k + 1):
+                nc.scalar.activation(out=unused[:], in_=diff[:, s, :], func=ACT.Abs, accum_out=dist[:, s:s + 1])
+            if len(step) > 1:
+                empty_bank(step[1][0], step[1][1], False)
             if k == 1:
-                nc.vector.tensor_reduce(out=dmin[:], in_=dist[:], axis=AX.X, op=ALU.min)
-                nc.vector.tensor_scalar(
-                    out=lg[:], in0=dist[:], scalar1=dmin[:], scalar2=rt1[:], op0=ALU.subtract, op1=ALU.mult
-                )
-            elif k == 2:
-                nc.scalar.activation(out=ex[:], in_=lg[:], func=ACT.Exp, scale=-1.0, accum_out=sume[:])
-            else:
-                nc.vector.reciprocal(out=rs[:], in_=sume[:])
-                nc.vector.tensor_scalar(out=attn[:], in0=ex[:], scalar1=rs[:], scalar2=None, op0=ALU.mult)
+                nc.vector.tensor_copy(out=z_obs_sb[:], in_=bank["Z"][:])
+                nc.vector.reciprocal(out=inv_t1[:], in_=t1_bf[:])
+                for g in GPSIMD_PAIRS:
+                    for s in (2 * g, 2 * g + 1):
+                        nc.gpsimd.tensor_tensor(
+                            out=diff[:, s, :], in0=c_sb[:, s, :], in1=z_obs_sb[:], op=ALU.subtract
+                        )
+            if k + AHEAD < len(BANK_STEPS):
+                for kind, j in BANK_STEPS[k + AHEAD]:
+                    transpose_bank(kind, j)
 
-        def mx(s, h):
-            bank["X", s] = psum.tile([P, N], F32, tag="ps", name="ps_x%d" % s)
+        def enc_frame(s):
+            target = new_bank(("X", s), "enc%d" % s)
             for t in range(2):
                 nc.tensor.matmul_mx(
-                    out=bank["X", s][:],
-                    lhsT=cc[:, (s + t) * P:(s + t + 1) * P].bitcast(FP8X4),
-                    lhsT_scale=cs[:, (s + t) * P:(s + t + 1) * P],
-                    rhs=wc[:, t, :].bitcast(FP8X4),
-                    rhs_scale=ws[:, t, :],
+                    out=target[:],
+                    lhsT=c_codes[:, (s + t) * P:(s + t + 1) * P].bitcast(FP8X4),
+                    lhsT_scale=c_scales[:, (s + t) * P:(s + t + 1) * P],
+                    rhs=w_codes[:, t, :].bitcast(FP8X4),
+                    rhs_scale=w_scales[:, t, :],
                     start=(t == 0),
                     stop=(t == 1),
                 )
 
-        def wsum(s, h):
+        for t in range(2):
+            nc.vector.quantize_mx(
+                out=w_codes[:, t, :].bitcast(FP8X4), scales=w_scales[:, t, :], in_=w_grouped[:, t, :]
+            )
+        started = 0
+        for s0 in range(0, LOADED, 4):
+            s1 = min(s0 + 4, LOADED)
+            nc.vector.quantize_mx(
+                out=c_codes[:, s0 * P:s1 * P].bitcast(FP8X4),
+                scales=c_scales[:, s0 * P:s1 * P],
+                in_=c_grouped[:, s0 * CH:s1 * CH],
+            )
+            ready = min(s1 - 1, PSUM_BANKS)
+            for s in range(started, ready):
+                enc_frame(s)
+            started = ready
+
+        least = keep.tile([P, 1], F32)
+        logit = keep.tile([P, FRAMES], F32)
+        expd = keep.tile([P, FRAMES], F32)
+        total = keep.tile([P, 1], F32)
+        inv_total = keep.tile([P, 1], F32)
+        attn = keep.tile([P, FRAMES], F32)
+        nc.vector.tensor_reduce(out=least[:], in_=dist[:], axis=AX.X, op=ALU.min)
+        nc.vector.tensor_scalar(
+            out=logit[:], in0=dist[:], scalar1=least[:], scalar2=inv_t1[:], op0=ALU.subtract, op1=ALU.mult
+        )
+        nc.scalar.activation(out=expd[:], in_=logit[:], func=ACT.Exp, scale=-1.0, accum_out=total[:])
+        nc.vector.reciprocal(out=inv_total[:], in_=total[:])
+        nc.vector.tensor_scalar(out=attn[:], in0=expd[:], scalar1=inv_total[:], scalar2=None, op0=ALU.mult)
+
+        sums = (keep.tile([P, CH], F32, name="sum_even"), keep.tile([P, CH], F32, name="sum_odd"))
+        sum_gpsimd = keep.tile([P, CH], F32)
+        weighted = keep.tile([P, len(SCALAR_FRAMES), CH], F32)
+        result = keep.tile([P, CH], F32)
+        for s in range(FRAMES):
             enc = bank["X", s]
-            a_s = attn[:, s:s + 1]
-            if s in WS_ON_SCALAR:
-                nc.scalar.activation(out=scaled[:, s, :], in_=enc[:], func=ACT.Copy, scale=a_s)
-                return
-            k = state["v_ws"]
-            state["v_ws"] = k + 1
-            if k == 0:
-                nc.vector.scalar_tensor_tensor(
-                    out=acc_a[:], in0=enc[:], scalar=a_s, in1=bias_bc[:], op0=ALU.mult, op1=ALU.add
-                )
-            elif k == 1:
-                nc.vector.tensor_scalar(out=acc_b[:], in0=enc[:], scalar1=a_s, scalar2=None, op0=ALU.mult)
+            weight = attn[:, s:s + 1]
+            if s in SCALAR_FRAMES:
+                k = SCALAR_FRAMES.index(s)
+                nc.scalar.activation(out=weighted[:, k, :], in_=enc[:], func=ACT.Copy, scale=weight)
+                if k > 0:
+                    nc.gpsimd.tensor_tensor(
+                        out=sum_gpsimd[:],
+                        in0=(weighted[:, 0, :] if k == 1 else sum_gpsimd[:]),
+                        in1=weighted[:, k, :],
+                        op=ALU.add,
+                    )
             else:
-                acc = acc_a if k % 2 == 0 else acc_b
-                nc.vector.scalar_tensor_tensor(
-                    out=acc[:], in0=enc[:], scalar=a_s, in1=acc[:], op0=ALU.mult, op1=ALU.add
-                )
-
-        def ga(s, h):
-            k = WS_ON_SCALAR.index(s)
-            prev = scaled[:, WS_ON_SCALAR[0], :] if k == 1 else acc_c[:]
-            nc.gpsimd.tensor_tensor(out=acc_c[:], in0=prev, in1=scaled[:, s, :], op=ALU.add)
-
-        def mg(k, h):
-            last = len(WS_ON_SCALAR) == 0 or k == 2
-            dst = res if last else acc_a
-            if k == 1:
-                nc.vector.tensor_tensor(out=dst[:], in0=acc_a[:], in1=acc_b[:], op=ALU.add)
-            else:
-                nc.vector.tensor_tensor(out=dst[:], in0=acc_a[:], in1=acc_c[:], op=ALU.add)
-            if last:
-                nc.sync.dma_start(out=out[:, :], in_=res[:])
-
-        funcs = {
-            "WM": wm, "GW": gw, "TD": td, "ED": ed, "MZ": mz, "TW": tw, "EW": ew, "QW": qw, "EZ": ez, "TC": tcx, "EC": ec,
-            "QC": qc, "SUB": sub, "ABS": absum, "RT": rt, "SM": sm, "MX": mx, "WS": wsum, "GA": ga, "MG": mg,
-        }
-        for kind, a, h in ORDER:
-            funcs[kind](a, h)
+                k = VECTOR_FRAMES.index(s)
+                acc = sums[k % 2]
+                if k == 1:
+                    nc.vector.tensor_scalar(out=acc[:], in0=enc[:], scalar1=weight, scalar2=None, op0=ALU.mult)
+                else:
+                    nc.vector.scalar_tensor_tensor(
+                        out=acc[:],
+                        in0=enc[:],
+                        scalar=weight,
+                        in1=(bias_bc[:] if k == 0 else acc[:]),
+                        op0=ALU.mult,
+                        op1=ALU.add,
+                    )
+            if s + PSUM_BANKS < FRAMES:
+                enc_frame(s + PSUM_BANKS)
+        nc.vector.tensor_tensor(out=sums[0][:], in0=sums[0][:], in1=sums[1][:], op=ALU.add)
+        nc.vector.tensor_tensor(out=result[:], in0=sums[0][:], in1=sum_gpsimd[:], op=ALU.add)
+        nc.sync.dma_start(out=out[:, :], in_=result[:])

@@ -33,6 +33,7 @@ BANK_STEPS = (
     (("C", 6), ("C", 7)),
     (("C", 8),),
 )
+IDLE_MATMULS = (4, 1, 2)
 AHEAD = 2
 
 
@@ -45,6 +46,8 @@ def tile_dynamix_pa_kernel(tc, context, D, z, conv_w, conv_b, t1, out):
 
         ident = keep.tile([P, P], F32)
         make_identity(nc, ident[:])
+        zeros = keep.tile([P, P], F32)
+        nc.vector.memset(zeros[:], 0.0)
 
         d_sb = keep.tile([P, 4, LATENT], BF16)
         z_sb = keep.tile([P, 4, 2, P], BF16)
@@ -112,10 +115,18 @@ def tile_dynamix_pa_kernel(tc, context, D, z, conv_w, conv_b, t1, out):
                     stop=(k == 7),
                 )
 
+        def keep_clock_up(count):
+            for i in range(count):
+                nc.tensor.matmul(bank["idle"][:, 0:P], lhsT=zeros[:], rhs=zeros[:], start=True, stop=True)
+
+        new_bank("idle", "idle")
         for c in range(4):
+            if c < 2:
+                keep_clock_up(IDLE_MATMULS[c])
             transpose_d(c)
             copy_d(c)
             if c == 1:
+                keep_clock_up(IDLE_MATMULS[2])
                 new_bank("Z", "z_obs")
             if c > 0:
                 z_obs_columns(c - 1)

from contextlib import ExitStack

import concourse.mybir as mybir
from concourse.masks import make_identity

F32 = mybir.dt.float32
BF16 = mybir.dt.bfloat16
U32 = mybir.dt.uint32
U8 = mybir.dt.uint8
FP8X4 = mybir.dt.float8_e4m3fn_x4
ALU = mybir.AluOpType
ACT = mybir.ActivationFunctionType
AX = mybir.AxisListType

P = 128
FRAMES = 16
LOADED = FRAMES + 1
CH = 512
LATENT = 1024
PAIRS = LOADED // 2
PSUM_BANKS = 8
FLOPS = 2 * FRAMES * P * CH * CH * 2 + 2 * CH * LATENT * P

GPSIMD_PAIRS = (6, 7)
SCALAR_FRAMES = (1, 4, 7, 10, 13)
VECTOR_FRAMES = tuple(s for s in range(FRAMES) if s not in SCALAR_FRAMES)
BANK_STEPS = (
    (("C", 0), ("C", 1)),
    (("W", 0), ("C", 2)),
    (("W", 1), ("C", 3)),
    (("W", 2), ("C", 4)),
    (("W", 3), ("C", 5)),
    (("C", 6), ("C", 7)),
    (("C", 8),),
)
IDLE_MATMULS = (4, 1, 2)
AHEAD = 2


def tile_dynamix_pa_kernel(tc, context, D, z, conv_w, conv_b, t1, out):
    nc = tc.nc
    with ExitStack() as stack:
        keep = stack.enter_context(tc.tile_pool(name="keep", bufs=1))
        psum = stack.enter_context(tc.psum_pool(name="psum", bufs=PSUM_BANKS))
        stack.enter_context(tc.manual_schedule())

        ident = keep.tile([P, P], F32)
        make_identity(nc, ident[:])
        zeros = keep.tile([P, P], F32)
        nc.vector.memset(zeros[:], 0.0)

        d_sb = keep.tile([P, 4, LATENT], BF16)
        z_sb = keep.tile([P, 4, 2, P], BF16)
        t1_bf = keep.tile([P, 1], BF16)
        c_sb = keep.tile([P, LOADED, CH], BF16)
        w_sb = keep.tile([P, 4, 2 * CH], BF16)
        bias_bc = keep.tile([P, CH], BF16)

        def load_d(c):
            nc.sync.dma_start(out=d_sb[:, c, :], in_=D[c * P:(c + 1) * P, :])

        def load_frames(g):
            s0, s1 = 2 * g, min(2 * g + 2, LOADED)
            nc.sync.dma_start(out=c_sb[:, s0:s1, :], in_=context[s0:s1].rearrange("s b i -> b s i"))

        load_d(0)
        load_d(1)
        nc.sync.dma_start(out=z_sb[:], in_=z.rearrange("(u q e) b -> q u e b", u=4, e=2))
        load_d(2)
        load_d(3)
        nc.sync.dma_start(out=t1_bf[:], in_=t1.partition_broadcast(P))
        load_frames(0)
        load_frames(1)
        for c in range(4):
            nc.sync.dma_start(out=w_sb[:, c, :], in_=conv_w[c * P:(c + 1) * P].rearrange("o i t -> o (i t)"))
        for g in range(2, PAIRS + 1):
            load_frames(g)
        nc.sync.dma_start(out=bias_bc[:], in_=conv_b.partition_broadcast(P))

        bank = {}

        def new_bank(key, name):
            bank[key] = psum.tile([P, CH], F32, tag="bank", name=name)
            return bank[key]

        d_t = keep.tile([P, 4 * CH], F32)
        d_t_words = d_t[:].rearrange("q (u i) -> q u i", u=4)
        d_t_halves = d_t[:].bitcast(BF16).rearrange("q (u i e) -> q u i e", u=4, e=2)

        def transpose_d(c):
            words = d_sb[:, c, :].bitcast(F32)
            for h in range(2):
                target = new_bank(("D", c, h), "d%d%d" % (c, h))
                for v in range(2):
                    u = 2 * h + v
                    nc.tensor.transpose(target[:, v * P:(v + 1) * P], words[:, u * P:(u + 1) * P], ident[:])

        def copy_d(c):
            cols = slice(c * P, (c + 1) * P)
            nc.vector.tensor_copy(
                out=d_t_words[:, 0:2, cols], in_=bank["D", c, 0][:, 0:2 * P].rearrange("q (u i) -> q u i", u=2)
            )
            nc.scalar.copy(
                out=d_t_words[:, 2:4, cols], in_=bank["D", c, 1][:, 0:2 * P].rearrange("q (u i) -> q u i", u=2)
            )

        def z_obs_columns(c):
            cols = slice(c * P, (c + 1) * P)
            for k in range(8):
                nc.tensor.matmul(
                    bank["Z"][:, cols],
                    lhsT=z_sb[:, k // 2, k % 2, :],
                    rhs=d_t_halves[:, k // 2, cols, k % 2],
                    start=(k == 0),
                    stop=(k == 7),
                )

        def keep_clock_up(count):
            for i in range(count):
                nc.tensor.matmul(bank["idle"][:, 0:P], lhsT=zeros[:], rhs=zeros[:], start=True, stop=True)

        new_bank("idle", "idle")
        for c in range(4):
            if c < 2:
                keep_clock_up(IDLE_MATMULS[c])
            transpose_d(c)
            copy_d(c)
            if c == 1:
                keep_clock_up(IDLE_MATMULS[2])
                new_bank("Z", "z_obs")
            if c > 0:
                z_obs_columns(c - 1)
        z_obs_columns(3)

        w_taps = keep.tile([P, 4, 2, CH], BF16)
        for c in range(4):
            nc.gpsimd.tensor_scalar(
                out=w_taps[:, c, :, :],
                in0=w_sb[:, c, :].rearrange("o (i t) -> o t i", t=2),
                scalar1=1.0,
                scalar2=0.0,
                op0=ALU.mult,
                op1=ALU.add,
            )

        c_grouped = keep.tile([P, LOADED * CH], BF16, align_bytes=64)
        c_codes = keep.tile([P, LOADED * P], U32, align_bytes=64)
        c_scales = keep.tile([P, LOADED * P], U8, align_bytes=64)
        w_grouped = keep.tile([P, 2, 4 * CH], BF16, align_bytes=64)
        w_codes = keep.tile([P, 2, CH], U32, align_bytes=64)
        w_scales = keep.tile([P, 2, CH], U8, align_bytes=64)
        w_grouped_words = (
            w_grouped[:].rearrange("q t k -> q (t k)").bitcast(F32).rearrange("q (t o u) -> q t o u", t=2, u=2)
        )

        def frames_of(g):
            return min(2, LOADED - 2 * g)

        def transpose_bank(kind, j):
            target = new_bank((kind, j), "%s%d" % (kind, j))
            for v in range(4 if kind == "W" else 2 * frames_of(j)):
                row = w_taps[:, j, v // 2, :] if kind == "W" else c_sb[:, 2 * j + v // 2, :]
                u = v % 2
                nc.tensor.transpose(target[:, v * P:(v + 1) * P], row.bitcast(F32)[:, u * P:(u + 1) * P], ident[:])

        def empty_bank(kind, j, on_scalar):
            if kind == "W":
                dst = w_grouped_words[:, :, j * P:(j + 1) * P, :]
                src = bank[kind, j][:].rearrange("q (t u o) -> q t o u", t=2, u=2)
            else:
                n = frames_of(j)
                dst = c_grouped[:, 2 * j * CH:(2 * j + n) * CH].bitcast(F32).rearrange(
                    "q (s b u) -> q s b u", s=n, u=2
                )
                src = bank[kind, j][:, 0:2 * n * P].rearrange("q (s u b) -> q s b u", s=n, u=2)
            if on_scalar:
                nc.scalar.copy(out=dst, in_=src)
            else:
                nc.vector.tensor_copy(out=dst, in_=src)

        z_obs_sb = keep.tile([P, CH], F32)
        diff = keep.tile([P, FRAMES, CH], F32)
        dist = keep.tile([P, FRAMES], F32)
        unused = keep.tile([P, CH], BF16)
        inv_t1 = keep.tile([P, 1], F32)

        for step in BANK_STEPS[0:AHEAD]:
            for kind, j in step:
                transpose_bank(kind, j)
        for k in range(PAIRS):
            step = BANK_STEPS[k] if k < len(BANK_STEPS) else ()
            if len(step) > 0:
                empty_bank(step[0][0], step[0][1], True)
            if k not in GPSIMD_PAIRS:
                nc.vector.tensor_tensor(
                    out=diff[:, 2 * k:2 * k + 2, :],
                    in0=c_sb[:, 2 * k:2 * k + 2, :],
                    in1=bank["Z"][:].unsqueeze(1).to_broadcast([P, 2, CH]),
                    op=ALU.subtract,
                )
            for s in (2 * k, 2 * k + 1):
                nc.scalar.activation(out=unused[:], in_=diff[:, s, :], func=ACT.Abs, accum_out=dist[:, s:s + 1])
            if len(step) > 1:
                empty_bank(step[1][0], step[1][1], False)
            if k == 1:
                nc.vector.tensor_copy(out=z_obs_sb[:], in_=bank["Z"][:])
                nc.vector.reciprocal(out=inv_t1[:], in_=t1_bf[:])
                for g in GPSIMD_PAIRS:
                    for s in (2 * g, 2 * g + 1):
                        nc.gpsimd.tensor_tensor(
                            out=diff[:, s, :], in0=c_sb[:, s, :], in1=z_obs_sb[:], op=ALU.subtract
                        )
            if k + AHEAD < len(BANK_STEPS):
                for kind, j in BANK_STEPS[k + AHEAD]:
                    transpose_bank(kind, j)

        def enc_frame(s):
            target = new_bank(("X", s), "enc%d" % s)
            for t in range(2):
                nc.tensor.matmul_mx(
                    out=target[:],
                    lhsT=c_codes[:, (s + t) * P:(s + t + 1) * P].bitcast(FP8X4),
                    lhsT_scale=c_scales[:, (s + t) * P:(s + t + 1) * P],
                    rhs=w_codes[:, t, :].bitcast(FP8X4),
                    rhs_scale=w_scales[:, t, :],
                    start=(t == 0),
                    stop=(t == 1),
                )

        for t in range(2):
            nc.vector.quantize_mx(
                out=w_codes[:, t, :].bitcast(FP8X4), scales=w_scales[:, t, :], in_=w_grouped[:, t, :]
            )
        started = 0
        for s0 in range(0, LOADED, 4):
            s1 = min(s0 + 4, LOADED)
            nc.vector.quantize_mx(
                out=c_codes[:, s0 * P:s1 * P].bitcast(FP8X4),
                scales=c_scales[:, s0 * P:s1 * P],
                in_=c_grouped[:, s0 * CH:s1 * CH],
            )
            ready = min(s1 - 1, PSUM_BANKS)
            for s in range(started, ready):
                enc_frame(s)
            started = ready

        least = keep.tile([P, 1], F32)
        logit = keep.tile([P, FRAMES], F32)
        expd = keep.tile([P, FRAMES], F32)
        total = keep.tile([P, 1], F32)
        inv_total = keep.tile([P, 1], F32)
        attn = keep.tile([P, FRAMES], F32)
        nc.vector.tensor_reduce(out=least[:], in_=dist[:], axis=AX.X, op=ALU.min)
        nc.vector.tensor_scalar(
            out=logit[:], in0=dist[:], scalar1=least[:], scalar2=inv_t1[:], op0=ALU.subtract, op1=ALU.mult
        )
        nc.scalar.activation(out=expd[:], in_=logit[:], func=ACT.Exp, scale=-1.0, accum_out=total[:])
        nc.vector.reciprocal(out=inv_total[:], in_=total[:])
        nc.vector.tensor_scalar(out=attn[:], in0=expd[:], scalar1=inv_total[:], scalar2=None, op0=ALU.mult)

        sums = (keep.tile([P, CH], F32, name="sum_even"), keep.tile([P, CH], F32, name="sum_odd"))
        sum_gpsimd = keep.tile([P, CH], F32)
        weighted = keep.tile([P, len(SCALAR_FRAMES), CH], F32)
        result = keep.tile([P, CH], F32)
        for s in range(FRAMES):
            enc = bank["X", s]
            weight = attn[:, s:s + 1]
            if s in SCALAR_FRAMES:
                k = SCALAR_FRAMES.index(s)
                nc.scalar.activation(out=weighted[:, k, :], in_=enc[:], func=ACT.Copy, scale=weight)
                if k > 0:
                    nc.gpsimd.tensor_tensor(
                        out=sum_gpsimd[:],
                        in0=(weighted[:, 0, :] if k == 1 else sum_gpsimd[:]),
                        in1=weighted[:, k, :],
                        op=ALU.add,
                    )
            else:
                k = VECTOR_FRAMES.index(s)
                acc = sums[k % 2]
                if k == 1:
                    nc.vector.tensor_scalar(out=acc[:], in0=enc[:], scalar1=weight, scalar2=None, op0=ALU.mult)
                else:
                    nc.vector.scalar_tensor_tensor(
                        out=acc[:],
                        in0=enc[:],
                        scalar=weight,
                        in1=(bias_bc[:] if k == 0 else acc[:]),
                        op0=ALU.mult,
                        op1=ALU.add,
                    )
            if s + PSUM_BANKS < FRAMES:
                enc_frame(s + PSUM_BANKS)
        nc.vector.tensor_tensor(out=sums[0][:], in0=sums[0][:], in1=sums[1][:], op=ALU.add)
        nc.vector.tensor_tensor(out=result[:], in0=sums[0][:], in1=sum_gpsimd[:], op=ALU.add)
        nc.sync.dma_start(out=out[:, :], in_=result[:])
